import numpy as np
import ml_dtypes


def mxq(x, axis, fmt="e4m3"):
    dtype, down = {"e4m3": (ml_dtypes.float8_e4m3fn, 7), "e5m2": (ml_dtypes.float8_e5m2, 14)}[fmt]
    v = np.moveaxis(np.asarray(x, np.float32).astype(ml_dtypes.bfloat16).astype(np.float64), axis, -1)
    blocks = v.reshape(v.shape[:-1] + (-1, 32))
    amax = np.abs(blocks).max(-1, keepdims=True)
    byte = np.maximum(np.where(amax > 0, np.frexp(amax)[1] - 1 + 127, 0) - down, 1)
    scale = np.exp2(byte - 127.0)
    codes = (blocks / scale).astype(np.float32).astype(dtype).astype(np.float64)
    return np.moveaxis((codes * scale).reshape(v.shape), -1, axis)


WIDE = False


def mx_kscale(k):
    if not WIDE:
        return np.ones(k)
    levels = np.array([10, -10, 5, -5, 0])
    if k % 512:
        return np.exp2(np.random.permutation(np.resize(levels, k // 32))).repeat(32)
    a = np.empty((k // 512, 16))
    for p in range(k // 512):
        a[p, :8] = np.random.permutation(np.resize(levels, 8))
        for g in range(8):
            far = levels[np.abs(levels - a[p, g]) >= 10]
            a[p, g + 8] = far[np.random.randint(len(far))]
    return np.exp2(a.ravel()).repeat(32)


BF16 = ml_dtypes.bfloat16


def bf(x):
    return np.asarray(x, np.float32).astype(BF16)


def f64(x):
    return np.asarray(x).astype(np.float64)


B, D, P, C, DEPTH = 4096, 1024, 512, 128, 2
INT = (1 << DEPTH) - 1
TOT = INT + INT + 1
SIGMA = 1.0


def path_probs(th):
    prob = np.ones((1, th.shape[1]))
    probs = [prob]
    off = 0
    for d in range(DEPTH):
        n = 1 << d
        t = th[off:off + n]
        left = prob * (1.0 + t) * 0.5
        right = prob * (1.0 - t) * 0.5
        prob = np.stack([left, right], axis=1).reshape(n + n, -1)
        probs.append(prob)
        off += n
    return np.concatenate(probs, axis=0)


def setup_inputs():
    s, t = mx_kscale(D), mx_kscale(P)
    return {"X": bf(np.random.standard_normal((B, D)) * s),
            "Z": bf(np.random.standard_normal((P, D)) * 0.25 * P / np.sqrt(D) * t[:, None] / s),
            "W": bf(np.random.standard_normal((C * TOT, P)) * 4.0 / np.sqrt(P) / t),
            "V": bf(np.random.standard_normal((C * TOT, P)) * 4.0 / np.sqrt(P) / t),
            "th": bf(np.tanh(1.5 * np.random.standard_normal((INT, B))))}


def reference(X, Z, W, V, th):
    Xp = (mxq(f64(Z), 1, "e4m3") @ mxq(f64(X), 1, "e4m3").T) / P
    Xq = mxq(Xp, 0, "e4m3")
    WX = (mxq(f64(W), 1, "e4m3") @ Xq).reshape(TOT, C, B)
    VX = (mxq(f64(V), 1, "e4m3") @ Xq).reshape(TOT, C, B)
    probs = path_probs(f64(th))
    return np.sum(probs[:, None, :] * WX * np.tanh(SIGMA * VX), axis=0)

@@ -1,0 +1,260 @@
+from contextlib import ExitStack
+
+import concourse.mybir as mybir
+from concourse.masks import make_identity
+
+F32 = mybir.dt.float32
+BF16 = mybir.dt.bfloat16
+U32 = mybir.dt.uint32
+U8 = mybir.dt.uint8
+FP8X4 = mybir.dt.float8_e4m3fn_x4
+ACT = mybir.ActivationFunctionType
+ALU = mybir.AluOpType
+
+P = 128
+PACK = 4
+K_PASS = P * PACK
+BANK = 512
+
+SAMPLES, FEATURES, PROJECTED, CLASSES = 4096, 1024, 512, 128
+INTERNAL, NODES = 3, 7
+SAMPLE_TILES = SAMPLES // P
+TILES_PER_LOAD = 4
+X_PASSES = FEATURES // K_PASS
+LOW_NODES = BANK // CLASSES
+
+LOW_WIDTHS = (512,)
+HIGH_WIDTHS = (256, 128)
+
+FOLDS = ((0, 3), (3, 2), (5, 1))
+
+X_LEAD = 4
+XP_LEAD = 2
+FOLD_LAG = 1
+OUT_LAG = 5
+
+FLOPS = 2 * PROJECTED * FEATURES * SAMPLES + 2 * 2 * NODES * CLASSES * PROJECTED * SAMPLES
+
+
+def tile_bonsailayer_pa_t_kernel(tc, X, Z, W, V, th, out):
+    nc = tc.nc
+    with ExitStack() as ctx:
+        keep = ctx.enter_context(tc.tile_pool(name="keep", bufs=1))
+        stage = ctx.enter_context(tc.tile_pool(name="stage", bufs=3))
+        codes_pool = ctx.enter_context(tc.tile_pool(name="codes", bufs=X_LEAD + 2))
+        work = ctx.enter_context(tc.tile_pool(name="work", bufs=3))
+        product_pool = ctx.enter_context(tc.tile_pool(name="product", bufs=OUT_LAG + 2))
+        words_psum = ctx.enter_context(tc.psum_pool(name="words_psum", bufs=2))
+        xp_psum = ctx.enter_context(tc.psum_pool(name="xp_psum", bufs=1))
+        vx_psum = ctx.enter_context(tc.psum_pool(name="vx_psum", bufs=2))
+        wx_psum = ctx.enter_context(tc.psum_pool(name="wx_psum", bufs=2))
+        out_psum = ctx.enter_context(tc.psum_pool(name="out_psum", bufs=1))
+        ctx.enter_context(tc.manual_schedule())
+
+        th_rows = keep.tile([P, P], BF16)
+        nc.vector.memset(th_rows[:], 0.0)
+        nc.sync.dma_start(
+            out=th_rows[0 : INTERNAL * SAMPLE_TILES, :],
+            in_=th.rearrange("n (i p) -> (n i) p", p=P),
+        )
+        z_rows = keep.tile([P, PACK, FEATURES], BF16)
+        nc.sync.dma_start(
+            out=z_rows[:],
+            in_=Z.rearrange("(p t) d -> p t d", t=PACK),
+        )
+        x_loads = X.rearrange("(g j p) d -> g p j d", j=TILES_PER_LOAD, p=P)
+        x_rows = []
+        for g in range(SAMPLE_TILES // TILES_PER_LOAD):
+            x_rows.append(keep.tile([P, TILES_PER_LOAD, FEATURES], BF16, name="x_rows%d" % g))
+        nc.sync.dma_start(out=x_rows[0][:], in_=x_loads[0])
+        vw_rows = keep.tile([P, 2 * NODES, PROJECTED], BF16)
+        nc.sync.dma_start(out=vw_rows[:, 0:NODES, :], in_=V.rearrange("(n p) k -> p n k", p=P))
+        nc.sync.dma_start(out=vw_rows[:, NODES:, :], in_=W.rearrange("(n p) k -> p n k", p=P))
+        for g in range(1, SAMPLE_TILES // TILES_PER_LOAD):
+            nc.sync.dma_start(out=x_rows[g][:], in_=x_loads[g])
+
+        identity = keep.tile([P, P], F32)
+        make_identity(nc, identity[:])
+
+        th_f32 = keep.tile([P, P], F32)
+        nc.vector.tensor_copy(out=th_f32[:], in_=th_rows[:])
+        th_bank = words_psum.tile([P, P], F32, tag="words")
+        nc.tensor.transpose(th_bank[:], th_f32[:], identity[:])
+        go_left = keep.tile([P, INTERNAL, SAMPLE_TILES], F32)
+        go_right = keep.tile([P, INTERNAL, SAMPLE_TILES], F32)
+        nc.vector.tensor_scalar(
+            out=go_left[:].rearrange("p n i -> p (n i)"), in0=th_bank[:, 0 : INTERNAL * SAMPLE_TILES],
+            scalar1=0.5, scalar2=0.5, op0=ALU.mult, op1=ALU.add,
+        )
+        nc.vector.tensor_scalar(
+            out=go_right[:].rearrange("p n i -> p (n i)"), in0=th_bank[:, 0 : INTERNAL * SAMPLE_TILES],
+            scalar1=-0.5, scalar2=0.5, op0=ALU.mult, op1=ALU.add,
+        )
+        prob = keep.tile([P, NODES, SAMPLE_TILES], F32)
+        nc.vector.memset(prob[:, 0, :], 1.0)
+        for n in range(INTERNAL):
+            nc.vector.tensor_tensor(
+                out=prob[:, 2 * n + 1, :], in0=prob[:, n, :], in1=go_left[:, n, :], op=ALU.mult
+            )
+            nc.vector.tensor_tensor(
+                out=prob[:, 2 * n + 2, :], in0=prob[:, n, :], in1=go_right[:, n, :], op=ALU.mult
+            )
+
+        def pair_blocks(words, passes):
+            return [words[:, 2 * P * c + u : 2 * P * (c + 1) : 2] for c in range(passes) for u in range(2)]
+
+        def quantise_four_blocks(blocks, codes, scales):
+            bank = words_psum.tile([P, 2, 2, P], F32, tag="words")
+            for slot in range(2):
+                for u in range(2):
+                    nc.tensor.transpose(bank[:, slot, u, :], blocks[2 * slot + u], identity[:])
+            grouped = stage.tile([P, 2 * P * PACK], BF16, tag="grouped", align_bytes=64)
+            nc.scalar.copy(
+                out=grouped[:].bitcast(F32).rearrange("p (s r u) -> p s r u", s=2, u=2),
+                in_=bank[:].rearrange("p s u r -> p s r u"),
+            )
+            nc.vector.quantize_mx(out=codes.bitcast(FP8X4), scales=scales, in_=grouped[:])
+
+        z_codes = keep.tile([P, PACK * X_PASSES * P], U32, align_bytes=64)
+        z_scales = keep.tile([P, PACK * X_PASSES * P], U8, align_bytes=64)
+        for t in range(PACK):
+            z_words = z_rows[:, t, :].bitcast(F32)
+            cols = slice(t * X_PASSES * P, (t + 1) * X_PASSES * P)
+            quantise_four_blocks(
+                pair_blocks(z_words, X_PASSES), z_codes[:, cols], z_scales[:, cols]
+            )
+
+        x_mx, xp_mx, products, out_banks = {}, {}, {}, {}
+
+        def quantise_x(i):
+            x_words = x_rows[i // TILES_PER_LOAD][:, i % TILES_PER_LOAD, :].bitcast(F32)
+            x_codes = codes_pool.tile([P, X_PASSES * P], U32, tag="x_codes", align_bytes=64)
+            x_scales = codes_pool.tile([P, X_PASSES * P], U8, tag="x_scales", align_bytes=64)
+            quantise_four_blocks(
+                pair_blocks(x_words, X_PASSES), x_codes[:], x_scales[:]
+            )
+            x_mx[i] = (x_codes, x_scales)
+
+        def project(i):
+            x_codes, x_scales = x_mx[i]
+            bank = xp_psum.tile([P, PACK, P], F32, tag="xp")
+            for t in range(PACK):
+                for c in range(X_PASSES):
+                    z_cols = slice((t * X_PASSES + c) * P, (t * X_PASSES + c + 1) * P)
+                    x_cols = slice(c * P, (c + 1) * P)
+                    nc.tensor.matmul_mx(
+                        out=bank[:, t, :],
+                        lhsT=z_codes[:, z_cols].bitcast(FP8X4),
+                        lhsT_scale=z_scales[:, z_cols],
+                        rhs=x_codes[:, x_cols].bitcast(FP8X4),
+                        rhs_scale=x_scales[:, x_cols],
+                        start=(c == 0),
+                        stop=(c == X_PASSES - 1),
+                    )
+            grouped = stage.tile([P, P, PACK], BF16, tag="xp_grouped", align_bytes=64)
+            nc.scalar.activation(
+                out=grouped[:], in_=bank[:].rearrange("p t b -> p b t"), func=ACT.Copy, scale=1.0 / PROJECTED
+            )
+            xp_codes = codes_pool.tile([P, P], U32, tag="xp_codes", align_bytes=64)
+            xp_scales = codes_pool.tile([P, P], U8, tag="xp_scales", align_bytes=64)
+            nc.vector.quantize_mx(
+                out=xp_codes[:].bitcast(FP8X4), scales=xp_scales[:], in_=grouped[:].rearrange("p b t -> p (b t)")
+            )
+            xp_mx[i] = (xp_codes, xp_scales)
+
+        def multiply_nodes(bank, i, first_row_tile, widths):
+            xp_codes, xp_scales = xp_mx[i]
+            done = 0
+            for width in widths:
+                vw_cols = slice(first_row_tile * P + done, first_row_tile * P + done + width)
+                nc.tensor.matmul_mx(
+                    out=bank[:, done : done + width],
+                    lhsT=xp_codes[:].bitcast(FP8X4),
+                    lhsT_scale=xp_scales[:],
+                    rhs=vw_codes[:, vw_cols].bitcast(FP8X4),
+                    rhs_scale=vw_scales[:, vw_cols],
+                    start=True,
+                    stop=True,
+                )
+                done += width
+
+        def score_nodes(i):
+            vx_low = vx_psum.tile([P, BANK], F32, tag="vx")
+            vx_high = vx_psum.tile([P, BANK], F32, tag="vx")
+            wx_low = wx_psum.tile([P, BANK], F32, tag="wx")
+            wx_high = wx_psum.tile([P, BANK], F32, tag="wx")
+            multiply_nodes(vx_low, i, 0, LOW_WIDTHS)
+            multiply_nodes(vx_high, i, LOW_NODES, HIGH_WIDTHS)
+            multiply_nodes(wx_low, i, NODES, LOW_WIDTHS)
+            multiply_nodes(wx_high, i, NODES + LOW_NODES, HIGH_WIDTHS)
+            tanh_vx = work.tile([P, NODES * CLASSES], F32, tag="tanh_vx")
+            nc.scalar.activation(out=tanh_vx[:, 0:BANK], in_=vx_low[:], func=ACT.Tanh)
+            nc.scalar.activation(
+                out=tanh_vx[:, BANK:], in_=vx_high[:, 0 : NODES * CLASSES - BANK], func=ACT.Tanh
+            )
+            product = product_pool.tile([P, NODES * CLASSES], F32, tag="product")
+            for n in range(NODES):
+                wx = wx_low if n < LOW_NODES else wx_high
+                bank_cols = slice((n % LOW_NODES) * CLASSES, (n % LOW_NODES + 1) * CLASSES)
+                node_cols = slice(n * CLASSES, (n + 1) * CLASSES)
+                nc.vector.scalar_tensor_tensor(
+                    out=product[:, node_cols],
+                    in0=wx[:, bank_cols],
+                    scalar=prob[:, n, i : i + 1],
+                    in1=tanh_vx[:, node_cols],
+                    op0=ALU.mult,
+                    op1=ALU.mult,
+                )
+            products[i] = product
+
+        def fold_nodes(i, first, count):
+            low = slice(first * CLASSES, (first + count) * CLASSES)
+            high = slice((first + count) * CLASSES, (first + 2 * count) * CLASSES)
+            nc.vector.tensor_tensor(
+                out=products[i][:, high], in0=products[i][:, low], in1=products[i][:, high], op=ALU.add
+            )
+
+        def transpose_score(i):
+            g, j = divmod(i, TILES_PER_LOAD)
+            if j == 0:
+                out_bank = out_psum.tile([P, TILES_PER_LOAD, P], F32, tag="out")
+                out_banks[g] = out_bank
+            nc.tensor.transpose(out_banks[g][:, j, :], products[i][:, (NODES - 1) * CLASSES :], identity[:])
+            if j == TILES_PER_LOAD - 1:
+                out_sb = work.tile([P, TILES_PER_LOAD * P], F32, tag="out_sb")
+                nc.scalar.copy(out=out_sb[:], in_=out_banks[g][:].rearrange("p j b -> p (j b)"))
+                nc.sync.dma_start(
+                    out=out[:, g * TILES_PER_LOAD * P : (g + 1) * TILES_PER_LOAD * P], in_=out_sb[:]
+                )
+
+        def is_tile(i):
+            return 0 <= i < SAMPLE_TILES
+
+        def pipeline_step(step):
+            if is_tile(step + X_LEAD):
+                quantise_x(step + X_LEAD)
+            if is_tile(step - OUT_LAG):
+                transpose_score(step - OUT_LAG)
+            if is_tile(step + XP_LEAD):
+                project(step + XP_LEAD)
+            if is_tile(step):
+                score_nodes(step)
+            for f, (first, count) in enumerate(FOLDS):
+                if is_tile(step - FOLD_LAG - f):
+                    fold_nodes(step - FOLD_LAG - f, first, count)
+
+        for step in range(-X_LEAD, 0):
+            pipeline_step(step)
+
+        vw_codes = keep.tile([P, 2 * NODES * P], U32, align_bytes=64)
+        vw_scales = keep.tile([P, 2 * NODES * P], U8, align_bytes=64)
+        for pair in range(NODES):
+            blocks = []
+            for r in (2 * pair, 2 * pair + 1):
+                vw_words = vw_rows[:, r, :].bitcast(F32)
+                blocks.extend(pair_blocks(vw_words, 1))
+            cols = slice(2 * pair * P, (2 * pair + 2) * P)
+            quantise_four_blocks(blocks, vw_codes[:, cols], vw_scales[:, cols])
+
+        for step in range(0, SAMPLE_TILES + OUT_LAG):
+            pipeline_step(step)

@@ -51,89 +51,75 @@ def tile_bonsailayer_pa_t_kernel(tc, X, Z, W, V, th, out):
         out_psum = ctx.enter_context(tc.psum_pool(name="out_psum", bufs=1))
         ctx.enter_context(tc.manual_schedule())
 
-        th_rows = keep.tile([P, P], BF16)
-        nc.vector.memset(th_rows[:], 0.0)
-        nc.sync.dma_start(
-            out=th_rows[0 : INTERNAL * SAMPLE_TILES, :],
-            in_=th.rearrange("n (i p) -> (n i) p", p=P),
-        )
         z_rows = keep.tile([P, PACK, FEATURES], BF16)
-        nc.sync.dma_start(
-            out=z_rows[:],
-            in_=Z.rearrange("(p t) d -> p t d", t=PACK),
-        )
+        z_loads = Z.rearrange("(p t) d -> p t d", t=PACK)
+        for t in range(PACK):
+            nc.sync.dma_start(out=z_rows[:, t, :], in_=z_loads[:, t, :])
         x_loads = X.rearrange("(g j p) d -> g p j d", j=TILES_PER_LOAD, p=P)
         x_rows = []
         for g in range(SAMPLE_TILES // TILES_PER_LOAD):
             x_rows.append(keep.tile([P, TILES_PER_LOAD, FEATURES], BF16, name="x_rows%d" % g))
-        nc.sync.dma_start(out=x_rows[0][:], in_=x_loads[0])
+        for j in range(TILES_PER_LOAD):
+            nc.sync.dma_start(out=x_rows[0][:, j, :], in_=x_loads[0][:, j, :])
         vw_rows = keep.tile([P, 2 * NODES, PROJECTED], BF16)
         nc.sync.dma_start(out=vw_rows[:, 0:NODES, :], in_=V.rearrange("(n p) k -> p n k", p=P))
         nc.sync.dma_start(out=vw_rows[:, NODES:, :], in_=W.rearrange("(n p) k -> p n k", p=P))
+        th_rows = keep.tile([P, P], BF16)
+        nc.gpsimd.memset(th_rows[:], 0.0)
+        nc.sync.dma_start(
+            out=th_rows[0 : INTERNAL * SAMPLE_TILES, :],
+            in_=th.rearrange("n (i p) -> (n i) p", p=P),
+        )
         for g in range(1, SAMPLE_TILES // TILES_PER_LOAD):
             nc.sync.dma_start(out=x_rows[g][:], in_=x_loads[g])
 
         identity = keep.tile([P, P], F32)
         make_identity(nc, identity[:])
-
-        th_f32 = keep.tile([P, P], F32)
-        nc.vector.tensor_copy(out=th_f32[:], in_=th_rows[:])
-        th_bank = words_psum.tile([P, P], F32, tag="words")
-        nc.tensor.transpose(th_bank[:], th_f32[:], identity[:])
-        go_left = keep.tile([P, INTERNAL, SAMPLE_TILES], F32)
-        go_right = keep.tile([P, INTERNAL, SAMPLE_TILES], F32)
-        nc.vector.tensor_scalar(
-            out=go_left[:].rearrange("p n i -> p (n i)"), in0=th_bank[:, 0 : INTERNAL * SAMPLE_TILES],
-            scalar1=0.5, scalar2=0.5, op0=ALU.mult, op1=ALU.add,
-        )
-        nc.vector.tensor_scalar(
-            out=go_right[:].rearrange("p n i -> p (n i)"), in0=th_bank[:, 0 : INTERNAL * SAMPLE_TILES],
-            scalar1=-0.5, scalar2=0.5, op0=ALU.mult, op1=ALU.add,
-        )
-        prob = keep.tile([P, NODES, SAMPLE_TILES], F32)
-        nc.vector.memset(prob[:, 0, :], 1.0)
-        for n in range(INTERNAL):
-            nc.vector.tensor_tensor(
-                out=prob[:, 2 * n + 1, :], in0=prob[:, n, :], in1=go_left[:, n, :], op=ALU.mult
-            )
-            nc.vector.tensor_tensor(
-                out=prob[:, 2 * n + 2, :], in0=prob[:, n, :], in1=go_right[:, n, :], op=ALU.mult
-            )
+        warm = keep.tile([P, 1], F32)
+        nc.vector.memset(warm[:], 0.0)
+        nc.scalar.activation(out=warm[:], in_=warm[:], func=ACT.Tanh)
 
         def pair_blocks(words, passes):
             return [words[:, 2 * P * c + u : 2 * P * (c + 1) : 2] for c in range(passes) for u in range(2)]
 
-        def quantise_four_blocks(blocks, codes, scales):
-            bank = words_psum.tile([P, 2, 2, P], F32, tag="words")
+        def transpose_blocks(bank, blocks):
             for slot in range(2):
                 for u in range(2):
                     nc.tensor.transpose(bank[:, slot, u, :], blocks[2 * slot + u], identity[:])
+
+        def group_words(bank, on_vector):
             grouped = stage.tile([P, 2 * P * PACK], BF16, tag="grouped", align_bytes=64)
-            nc.scalar.copy(
+            copy = nc.vector.tensor_copy if on_vector else nc.scalar.copy
+            copy(
                 out=grouped[:].bitcast(F32).rearrange("p (s r u) -> p s r u", s=2, u=2),
                 in_=bank[:].rearrange("p s u r -> p s r u"),
             )
+            return grouped
+
+        def quantise(grouped, codes, scales):
             nc.vector.quantize_mx(out=codes.bitcast(FP8X4), scales=scales, in_=grouped[:])
 
         z_codes = keep.tile([P, PACK * X_PASSES * P], U32, align_bytes=64)
         z_scales = keep.tile([P, PACK * X_PASSES * P], U8, align_bytes=64)
-        for t in range(PACK):
-            z_words = z_rows[:, t, :].bitcast(F32)
-            cols = slice(t * X_PASSES * P, (t + 1) * X_PASSES * P)
-            quantise_four_blocks(
-                pair_blocks(z_words, X_PASSES), z_codes[:, cols], z_scales[:, cols]
-            )
+        vw_codes = keep.tile([P, 2 * NODES * P], U32, align_bytes=64)
+        vw_scales = keep.tile([P, 2 * NODES * P], U8, align_bytes=64)
 
         x_mx, xp_mx, products, out_banks = {}, {}, {}, {}
 
-        def quantise_x(i):
-            x_words = x_rows[i // TILES_PER_LOAD][:, i % TILES_PER_LOAD, :].bitcast(F32)
+        def x_blocks(i):
+            return pair_blocks(x_rows[i // TILES_PER_LOAD][:, i % TILES_PER_LOAD, :].bitcast(F32), X_PASSES)
+
+        def x_operand(i):
             x_codes = codes_pool.tile([P, X_PASSES * P], U32, tag="x_codes", align_bytes=64)
             x_scales = codes_pool.tile([P, X_PASSES * P], U8, tag="x_scales", align_bytes=64)
-            quantise_four_blocks(
-                pair_blocks(x_words, X_PASSES), x_codes[:], x_scales[:]
-            )
             x_mx[i] = (x_codes, x_scales)
+            return x_codes[:], x_scales[:]
+
+        def quantise_x(i):
+            bank = words_psum.tile([P, 2, 2, P], F32, tag="words")
+            transpose_blocks(bank, x_blocks(i))
+            codes, scales = x_operand(i)
+            quantise(group_words(bank, False), codes, scales)
 
         def project(i):
             x_codes, x_scales = x_mx[i]
@@ -243,18 +229,62 @@ def tile_bonsailayer_pa_t_kernel(tc, X, Z, W, V, th, out):
                 if is_tile(step - FOLD_LAG - f):
                     fold_nodes(step - FOLD_LAG - f, first, count)
 
-        for step in range(-X_LEAD, 0):
-            pipeline_step(step)
+        head_banks = [(words_psum, "words"), (vx_psum, "vx"), (wx_psum, "wx")]
+        units_done = []
+        waiting = []
 
-        vw_codes = keep.tile([P, 2 * NODES * P], U32, align_bytes=64)
-        vw_scales = keep.tile([P, 2 * NODES * P], U8, align_bytes=64)
+        def head_unit(blocks, codes, scales):
+            n = len(units_done)
+            units_done.append(n)
+            pool, tag = head_banks[n % 3]
+            bank = pool.tile([P, 2, 2, P], F32, tag=tag, name="head_bank")
+            transpose_blocks(bank, blocks)
+            waiting.append((group_words(bank, n % 3 == 2), codes, scales))
+            if len(waiting) > 1:
+                quantise(*waiting.pop(0))
+
+        for t in range(PACK):
+            cols = slice(t * X_PASSES * P, (t + 1) * X_PASSES * P)
+            head_unit(pair_blocks(z_rows[:, t, :].bitcast(F32), X_PASSES), z_codes[:, cols], z_scales[:, cols])
+        for i in range(X_LEAD):
+            codes, scales = x_operand(i)
+            head_unit(x_blocks(i), codes, scales)
         for pair in range(NODES):
+            if pair == LOW_NODES:
+                for i in range(XP_LEAD):
+                    project(i)
             blocks = []
             for r in (2 * pair, 2 * pair + 1):
-                vw_words = vw_rows[:, r, :].bitcast(F32)
-                blocks.extend(pair_blocks(vw_words, 1))
+                blocks.extend(pair_blocks(vw_rows[:, r, :].bitcast(F32), 1))
             cols = slice(2 * pair * P, (2 * pair + 2) * P)
-            quantise_four_blocks(blocks, vw_codes[:, cols], vw_scales[:, cols])
+            head_unit(blocks, vw_codes[:, cols], vw_scales[:, cols])
+        quantise(*waiting.pop(0))
+
+        th_f32 = keep.tile([P, P], F32)
+        nc.gpsimd.tensor_copy(out=th_f32[:], in_=th_rows[:])
+        th_bank = words_psum.tile([P, P], F32, tag="words")
+        nc.tensor.transpose(th_bank[:], th_f32[:], identity[:])
+        th_cols = keep.tile([P, INTERNAL, SAMPLE_TILES], F32)
+        nc.scalar.copy(
+            out=th_cols[:].rearrange("p n i -> p (n i)"), in_=th_bank[:, 0 : INTERNAL * SAMPLE_TILES]
+        )
+        go_left = keep.tile([P, INTERNAL, SAMPLE_TILES], F32)
+        go_right = keep.tile([P, INTERNAL, SAMPLE_TILES], F32)
+        nc.gpsimd.tensor_scalar(
+            out=go_left[:], in0=th_cols[:], scalar1=0.5, scalar2=0.5, op0=ALU.mult, op1=ALU.add
+        )
+        nc.gpsimd.tensor_scalar(
+            out=go_right[:], in0=th_cols[:], scalar1=-0.5, scalar2=0.5, op0=ALU.mult, op1=ALU.add
+        )
+        prob = keep.tile([P, NODES, SAMPLE_TILES], F32)
+        nc.gpsimd.memset(prob[:, 0, :], 1.0)
+        for n in range(INTERNAL):
+            nc.gpsimd.tensor_tensor(
+                out=prob[:, 2 * n + 1, :], in0=prob[:, n, :], in1=go_left[:, n, :], op=ALU.mult
+            )
+            nc.gpsimd.tensor_tensor(
+                out=prob[:, 2 * n + 2, :], in0=prob[:, n, :], in1=go_right[:, n, :], op=ALU.mult
+            )
 
         for step in range(0, SAMPLE_TILES + OUT_LAG):
             pipeline_step(step)

@@ -28,10 +28,11 @@ HIGH_WIDTHS = (256, 128)
 
 FOLDS = ((0, 3), (3, 2), (5, 1))
 
-X_LEAD = 4
-XP_LEAD = 2
-FOLD_LAG = 1
-OUT_LAG = 5
+GROUP = 2
+GROUPS = SAMPLE_TILES // GROUP
+X_LEAD = 2
+XP_LEAD = 1
+OUT_LAG = 2
 
 FLOPS = 2 * PROJECTED * FEATURES * SAMPLES + 2 * 2 * NODES * CLASSES * PROJECTED * SAMPLES
 
@@ -41,14 +42,12 @@ def tile_bonsailayer_pa_t_kernel(tc, X, Z, W, V, th, out):
     with ExitStack() as ctx:
         keep = ctx.enter_context(tc.tile_pool(name="keep", bufs=1))
         stage = ctx.enter_context(tc.tile_pool(name="stage", bufs=3))
-        codes_pool = ctx.enter_context(tc.tile_pool(name="codes", bufs=X_LEAD + 2))
+        codes_pool = ctx.enter_context(tc.tile_pool(name="codes", bufs=GROUP * (X_LEAD + 1)))
         work = ctx.enter_context(tc.tile_pool(name="work", bufs=3))
         product_pool = ctx.enter_context(tc.tile_pool(name="product", bufs=OUT_LAG + 2))
         words_psum = ctx.enter_context(tc.psum_pool(name="words_psum", bufs=2))
-        xp_psum = ctx.enter_context(tc.psum_pool(name="xp_psum", bufs=1))
-        vx_psum = ctx.enter_context(tc.psum_pool(name="vx_psum", bufs=2))
-        wx_psum = ctx.enter_context(tc.psum_pool(name="wx_psum", bufs=2))
-        out_psum = ctx.enter_context(tc.psum_pool(name="out_psum", bufs=1))
+        xp_psum = ctx.enter_context(tc.psum_pool(name="xp_psum", bufs=2))
+        nodes_psum = ctx.enter_context(tc.psum_pool(name="nodes_psum", bufs=1))
         ctx.enter_context(tc.manual_schedule())
 
         z_rows = keep.tile([P, PACK, FEATURES], BF16)
@@ -61,15 +60,15 @@ def tile_bonsailayer_pa_t_kernel(tc, X, Z, W, V, th, out):
             x_rows.append(keep.tile([P, TILES_PER_LOAD, FEATURES], BF16, name="x_rows%d" % g))
         for j in range(TILES_PER_LOAD):
             nc.sync.dma_start(out=x_rows[0][:, j, :], in_=x_loads[0][:, j, :])
-        vw_rows = keep.tile([P, 2 * NODES, PROJECTED], BF16)
-        nc.sync.dma_start(out=vw_rows[:, 0:NODES, :], in_=V.rearrange("(n p) k -> p n k", p=P))
-        nc.sync.dma_start(out=vw_rows[:, NODES:, :], in_=W.rearrange("(n p) k -> p n k", p=P))
         th_rows = keep.tile([P, P], BF16)
         nc.gpsimd.memset(th_rows[:], 0.0)
         nc.sync.dma_start(
             out=th_rows[0 : INTERNAL * SAMPLE_TILES, :],
             in_=th.rearrange("n (i p) -> (n i) p", p=P),
         )
+        vw_rows = keep.tile([P, 2 * NODES, PROJECTED], BF16)
+        nc.sync.dma_start(out=vw_rows[:, 0:NODES, :], in_=V.rearrange("(n p) k -> p n k", p=P))
+        nc.sync.dma_start(out=vw_rows[:, NODES:, :], in_=W.rearrange("(n p) k -> p n k", p=P))
         for g in range(1, SAMPLE_TILES // TILES_PER_LOAD):
             nc.sync.dma_start(out=x_rows[g][:], in_=x_loads[g])
 
@@ -104,7 +103,7 @@ def tile_bonsailayer_pa_t_kernel(tc, X, Z, W, V, th, out):
         vw_codes = keep.tile([P, 2 * NODES * P], U32, align_bytes=64)
         vw_scales = keep.tile([P, 2 * NODES * P], U8, align_bytes=64)
 
-        x_mx, xp_mx, products, out_banks = {}, {}, {}, {}
+        x_mx, xp_banks, xp_mx, node_banks, products = {}, {}, {}, {}, {}
 
         def x_blocks(i):
             return pair_blocks(x_rows[i // TILES_PER_LOAD][:, i % TILES_PER_LOAD, :].bitcast(F32), X_PASSES)
@@ -115,11 +114,10 @@ def tile_bonsailayer_pa_t_kernel(tc, X, Z, W, V, th, out):
             x_mx[i] = (x_codes, x_scales)
             return x_codes[:], x_scales[:]
 
-        def quantise_x(i):
+        def transpose_x(i):
             bank = words_psum.tile([P, 2, 2, P], F32, tag="words")
             transpose_blocks(bank, x_blocks(i))
-            codes, scales = x_operand(i)
-            quantise(group_words(bank, False), codes, scales)
+            return bank
 
         def project(i):
             x_codes, x_scales = x_mx[i]
@@ -137,10 +135,16 @@ def tile_bonsailayer_pa_t_kernel(tc, X, Z, W, V, th, out):
                         start=(c == 0),
                         stop=(c == X_PASSES - 1),
                     )
+            xp_banks[i] = bank
+
+        def group_xp(i):
             grouped = stage.tile([P, P, PACK], BF16, tag="xp_grouped", align_bytes=64)
             nc.scalar.activation(
-                out=grouped[:], in_=bank[:].rearrange("p t b -> p b t"), func=ACT.Copy, scale=1.0 / PROJECTED
+                out=grouped[:], in_=xp_banks[i][:].rearrange("p t b -> p b t"), func=ACT.Copy, scale=1.0 / PROJECTED
             )
+            return grouped
+
+        def quantise_xp(i, grouped):
             xp_codes = codes_pool.tile([P, P], U32, tag="xp_codes", align_bytes=64)
             xp_scales = codes_pool.tile([P, P], U8, tag="xp_scales", align_bytes=64)
             nc.vector.quantize_mx(
@@ -164,79 +168,143 @@ def tile_bonsailayer_pa_t_kernel(tc, X, Z, W, V, th, out):
                 )
                 done += width
 
-        def score_nodes(i):
-            vx_low = vx_psum.tile([P, BANK], F32, tag="vx")
-            vx_high = vx_psum.tile([P, BANK], F32, tag="vx")
-            wx_low = wx_psum.tile([P, BANK], F32, tag="wx")
-            wx_high = wx_psum.tile([P, BANK], F32, tag="wx")
+        def multiply_all_nodes(i):
+            vx_low = nodes_psum.tile([P, BANK], F32, tag="vx_low")
+            vx_high = nodes_psum.tile([P, BANK], F32, tag="vx_high")
+            wx_low = nodes_psum.tile([P, BANK], F32, tag="wx_low")
+            wx_high = nodes_psum.tile([P, BANK], F32, tag="wx_high")
             multiply_nodes(vx_low, i, 0, LOW_WIDTHS)
             multiply_nodes(vx_high, i, LOW_NODES, HIGH_WIDTHS)
             multiply_nodes(wx_low, i, NODES, LOW_WIDTHS)
             multiply_nodes(wx_high, i, NODES + LOW_NODES, HIGH_WIDTHS)
+            node_banks[i] = (vx_low, vx_high, wx_low, wx_high)
+
+        def tanh_nodes(i):
+            vx_low, vx_high, wx_low, wx_high = node_banks[i]
             tanh_vx = work.tile([P, NODES * CLASSES], F32, tag="tanh_vx")
             nc.scalar.activation(out=tanh_vx[:, 0:BANK], in_=vx_low[:], func=ACT.Tanh)
             nc.scalar.activation(
                 out=tanh_vx[:, BANK:], in_=vx_high[:, 0 : NODES * CLASSES - BANK], func=ACT.Tanh
             )
-            product = product_pool.tile([P, NODES * CLASSES], F32, tag="product")
+            node_banks[i] = (tanh_vx, wx_low, wx_high)
+
+        def multiply_tanh(i):
+            tanh_vx, wx_low, wx_high = node_banks[i]
+            s, j = divmod(i, GROUP)
+            if j == 0:
+                product = product_pool.tile([P, GROUP, NODES * CLASSES], F32, tag="product")
+                products[s] = product
             for n in range(NODES):
                 wx = wx_low if n < LOW_NODES else wx_high
                 bank_cols = slice((n % LOW_NODES) * CLASSES, (n % LOW_NODES + 1) * CLASSES)
                 node_cols = slice(n * CLASSES, (n + 1) * CLASSES)
                 nc.vector.scalar_tensor_tensor(
-                    out=product[:, node_cols],
+                    out=products[s][:, j, node_cols],
                     in0=wx[:, bank_cols],
                     scalar=prob[:, n, i : i + 1],
                     in1=tanh_vx[:, node_cols],
                     op0=ALU.mult,
                     op1=ALU.mult,
                 )
-            products[i] = product
 
-        def fold_nodes(i, first, count):
+        def fold_nodes(s, f):
+            first, count = FOLDS[f]
             low = slice(first * CLASSES, (first + count) * CLASSES)
             high = slice((first + count) * CLASSES, (first + 2 * count) * CLASSES)
             nc.vector.tensor_tensor(
-                out=products[i][:, high], in0=products[i][:, low], in1=products[i][:, high], op=ALU.add
+                out=products[s][:, :, high], in0=products[s][:, :, low], in1=products[s][:, :, high], op=ALU.add
             )
 
-        def transpose_score(i):
-            g, j = divmod(i, TILES_PER_LOAD)
-            if j == 0:
-                out_bank = out_psum.tile([P, TILES_PER_LOAD, P], F32, tag="out")
-                out_banks[g] = out_bank
-            nc.tensor.transpose(out_banks[g][:, j, :], products[i][:, (NODES - 1) * CLASSES :], identity[:])
-            if j == TILES_PER_LOAD - 1:
-                out_sb = work.tile([P, TILES_PER_LOAD * P], F32, tag="out_sb")
-                nc.scalar.copy(out=out_sb[:], in_=out_banks[g][:].rearrange("p j b -> p (j b)"))
-                nc.sync.dma_start(
-                    out=out[:, g * TILES_PER_LOAD * P : (g + 1) * TILES_PER_LOAD * P], in_=out_sb[:]
+        def transpose_score(s):
+            bank = words_psum.tile([P, GROUP, P], F32, tag="words", name="out_bank")
+            for j in range(GROUP):
+                nc.tensor.transpose(bank[:, j, :], products[s][:, j, (NODES - 1) * CLASSES :], identity[:])
+            return bank
+
+        def store_score(s, bank):
+            out_sb = work.tile([P, GROUP * P], F32, tag="out_sb")
+            nc.scalar.copy(out=out_sb[:], in_=bank[:].rearrange("p j b -> p (j b)"))
+            nc.sync.dma_start(out=out[:, s * GROUP * P : (s + 1) * GROUP * P], in_=out_sb[:])
+
+        def is_group(s):
+            return 0 <= s < GROUPS
+
+        def pipeline_step(s):
+            a, b = GROUP * s, GROUP * s + 1
+            if is_group(s - OUT_LAG):
+                out_bank = transpose_score(s - OUT_LAG)
+            x_ahead = []
+            if is_group(s + X_LEAD):
+                x_ahead = [(i, transpose_x(i)) for i in (a + GROUP * X_LEAD, b + GROUP * X_LEAD)]
+            if is_group(s - OUT_LAG):
+                store_score(s - OUT_LAG, out_bank)
+            if is_group(s):
+                xp_b = group_xp(b)
+            x_grouped = [(i, group_words(bank, False)) for i, bank in x_ahead]
+
+            if is_group(s - 1):
+                multiply_tanh(b - GROUP)
+            if is_group(s):
+                quantise_xp(b, xp_b)
+            if is_group(s - 1):
+                fold_nodes(s - 1, 0)
+            for i, grouped in x_grouped[:1]:
+                quantise(grouped, *x_operand(i))
+            if is_group(s - 1):
+                fold_nodes(s - 1, 1)
+
+            if is_group(s):
+                multiply_all_nodes(a)
+                tanh_nodes(a)
+                multiply_tanh(a)
+            if is_group(s - 1):
+                fold_nodes(s - 1, 2)
+            for i, grouped in x_grouped[1:]:
+                quantise(grouped, *x_operand(i))
+            if is_group(s + XP_LEAD):
+                project(a + GROUP * XP_LEAD)
+                project(b + GROUP * XP_LEAD)
+                quantise_xp(a + GROUP * XP_LEAD, group_xp(a + GROUP * XP_LEAD))
+            if is_group(s):
+                multiply_all_nodes(b)
+                tanh_nodes(b)
+
+        prob = keep.tile([P, NODES, SAMPLE_TILES], F32)
+
+        def path_probabilities():
+            th_f32 = keep.tile([P, P], F32)
+            nc.gpsimd.tensor_copy(out=th_f32[:], in_=th_rows[:])
+            th_bank = words_psum.tile([P, P], F32, tag="words")
+            nc.tensor.transpose(th_bank[:], th_f32[:], identity[:])
+            th_cols = keep.tile([P, INTERNAL, SAMPLE_TILES], F32)
+            nc.scalar.copy(
+                out=th_cols[:].rearrange("p n i -> p (n i)"), in_=th_bank[:, 0 : INTERNAL * SAMPLE_TILES]
+            )
+            go_left = keep.tile([P, INTERNAL, SAMPLE_TILES], F32)
+            go_right = keep.tile([P, INTERNAL, SAMPLE_TILES], F32)
+            nc.gpsimd.tensor_scalar(
+                out=go_left[:], in0=th_cols[:], scalar1=0.5, scalar2=0.5, op0=ALU.mult, op1=ALU.add
+            )
+            nc.gpsimd.tensor_scalar(
+                out=go_right[:], in0=th_cols[:], scalar1=-0.5, scalar2=0.5, op0=ALU.mult, op1=ALU.add
+            )
+            nc.gpsimd.memset(prob[:, 0, :], 1.0)
+            for n in range(INTERNAL):
+                nc.gpsimd.tensor_tensor(
+                    out=prob[:, 2 * n + 1, :], in0=prob[:, n, :], in1=go_left[:, n, :], op=ALU.mult
+                )
+                nc.gpsimd.tensor_tensor(
+                    out=prob[:, 2 * n + 2, :], in0=prob[:, n, :], in1=go_right[:, n, :], op=ALU.mult
                 )
 
-        def is_tile(i):
-            return 0 <= i < SAMPLE_TILES
-
-        def pipeline_step(step):
-            if is_tile(step + X_LEAD):
-                quantise_x(step + X_LEAD)
-            if is_tile(step - OUT_LAG):
-                transpose_score(step - OUT_LAG)
-            if is_tile(step + XP_LEAD):
-                project(step + XP_LEAD)
-            if is_tile(step):
-                score_nodes(step)
-            for f, (first, count) in enumerate(FOLDS):
-                if is_tile(step - FOLD_LAG - f):
-                    fold_nodes(step - FOLD_LAG - f, first, count)
-
-        head_banks = [(words_psum, "words"), (vx_psum, "vx"), (wx_psum, "wx")]
+        head_banks = [(words_psum, "words"), (nodes_psum, "vx_low"), (nodes_psum, "vx_high"), (words_psum, "words"), (nodes_psum, "wx_low"), (nodes_psum, "wx_high")]
         units_done = []
         waiting = []
 
         def head_unit(blocks, codes, scales):
             n = len(units_done)
             units_done.append(n)
-            pool, tag = head_banks[n % 3]
+            pool, tag = head_banks[n % 6]
             bank = pool.tile([P, 2, 2, P], F32, tag=tag, name="head_bank")
             transpose_blocks(bank, blocks)
             waiting.append((group_words(bank, n % 3 == 2), codes, scales))
@@ -246,45 +314,22 @@ def tile_bonsailayer_pa_t_kernel(tc, X, Z, W, V, th, out):
         for t in range(PACK):
             cols = slice(t * X_PASSES * P, (t + 1) * X_PASSES * P)
             head_unit(pair_blocks(z_rows[:, t, :].bitcast(F32), X_PASSES), z_codes[:, cols], z_scales[:, cols])
-        for i in range(X_LEAD):
+        for i in range(GROUP * X_LEAD):
             codes, scales = x_operand(i)
             head_unit(x_blocks(i), codes, scales)
         for pair in range(NODES):
             if pair == LOW_NODES:
-                for i in range(XP_LEAD):
+                for i in range(GROUP * XP_LEAD):
                     project(i)
+                xp_a = group_xp(0)
+                path_probabilities()
             blocks = []
             for r in (2 * pair, 2 * pair + 1):
                 blocks.extend(pair_blocks(vw_rows[:, r, :].bitcast(F32), 1))
             cols = slice(2 * pair * P, (2 * pair + 2) * P)
             head_unit(blocks, vw_codes[:, cols], vw_scales[:, cols])
         quantise(*waiting.pop(0))
+        quantise_xp(0, xp_a)
 
-        th_f32 = keep.tile([P, P], F32)
-        nc.gpsimd.tensor_copy(out=th_f32[:], in_=th_rows[:])
-        th_bank = words_psum.tile([P, P], F32, tag="words")
-        nc.tensor.transpose(th_bank[:], th_f32[:], identity[:])
-        th_cols = keep.tile([P, INTERNAL, SAMPLE_TILES], F32)
-        nc.scalar.copy(
-            out=th_cols[:].rearrange("p n i -> p (n i)"), in_=th_bank[:, 0 : INTERNAL * SAMPLE_TILES]
-        )
-        go_left = keep.tile([P, INTERNAL, SAMPLE_TILES], F32)
-        go_right = keep.tile([P, INTERNAL, SAMPLE_TILES], F32)
-        nc.gpsimd.tensor_scalar(
-            out=go_left[:], in0=th_cols[:], scalar1=0.5, scalar2=0.5, op0=ALU.mult, op1=ALU.add
-        )
-        nc.gpsimd.tensor_scalar(
-            out=go_right[:], in0=th_cols[:], scalar1=-0.5, scalar2=0.5, op0=ALU.mult, op1=ALU.add
-        )
-        prob = keep.tile([P, NODES, SAMPLE_TILES], F32)
-        nc.gpsimd.memset(prob[:, 0, :], 1.0)
-        for n in range(INTERNAL):
-            nc.gpsimd.tensor_tensor(
-                out=prob[:, 2 * n + 1, :], in0=prob[:, n, :], in1=go_left[:, n, :], op=ALU.mult
-            )
-            nc.gpsimd.tensor_tensor(
-                out=prob[:, 2 * n + 2, :], in0=prob[:, n, :], in1=go_right[:, n, :], op=ALU.mult
-            )
-
-        for step in range(0, SAMPLE_TILES + OUT_LAG):
-            pipeline_step(step)
+        for s in range(GROUPS + OUT_LAG):
+            pipeline_step(s)

@@ -103,7 +103,7 @@ def tile_bonsailayer_pa_t_kernel(tc, X, Z, W, V, th, out):
         vw_codes = keep.tile([P, 2 * NODES * P], U32, align_bytes=64)
         vw_scales = keep.tile([P, 2 * NODES * P], U8, align_bytes=64)
 
-        x_mx, xp_banks, xp_mx, node_banks, products = {}, {}, {}, {}, {}
+        x_mx, xp_banks, xp_grouped, xp_mx, node_banks, products = {}, {}, {}, {}, {}, {}
 
         def x_blocks(i):
             return pair_blocks(x_rows[i // TILES_PER_LOAD][:, i % TILES_PER_LOAD, :].bitcast(F32), X_PASSES)
@@ -142,13 +142,13 @@ def tile_bonsailayer_pa_t_kernel(tc, X, Z, W, V, th, out):
             nc.scalar.activation(
                 out=grouped[:], in_=xp_banks[i][:].rearrange("p t b -> p b t"), func=ACT.Copy, scale=1.0 / PROJECTED
             )
-            return grouped
+            xp_grouped[i] = grouped
 
-        def quantise_xp(i, grouped):
+        def quantise_xp(i):
             xp_codes = codes_pool.tile([P, P], U32, tag="xp_codes", align_bytes=64)
             xp_scales = codes_pool.tile([P, P], U8, tag="xp_scales", align_bytes=64)
             nc.vector.quantize_mx(
-                out=xp_codes[:].bitcast(FP8X4), scales=xp_scales[:], in_=grouped[:].rearrange("p b t -> p (b t)")
+                out=xp_codes[:].bitcast(FP8X4), scales=xp_scales[:], in_=xp_grouped[i][:].rearrange("p b t -> p (b t)")
             )
             xp_mx[i] = (xp_codes, xp_scales)
 
@@ -216,7 +216,7 @@ def tile_bonsailayer_pa_t_kernel(tc, X, Z, W, V, th, out):
             )
 
         def transpose_score(s):
-            bank = words_psum.tile([P, GROUP, P], F32, tag="words", name="out_bank")
+            bank = xp_psum.tile([P, GROUP, P], F32, tag="xp", name="out_bank")
             for j in range(GROUP):
                 nc.tensor.transpose(bank[:, j, :], products[s][:, j, (NODES - 1) * CLASSES :], identity[:])
             return bank
@@ -231,25 +231,24 @@ def tile_bonsailayer_pa_t_kernel(tc, X, Z, W, V, th, out):
 
         def pipeline_step(s):
             a, b = GROUP * s, GROUP * s + 1
+            xa, xb = a + GROUP * X_LEAD, b + GROUP * X_LEAD
             if is_group(s - OUT_LAG):
                 out_bank = transpose_score(s - OUT_LAG)
-            x_ahead = []
             if is_group(s + X_LEAD):
-                x_ahead = [(i, transpose_x(i)) for i in (a + GROUP * X_LEAD, b + GROUP * X_LEAD)]
+                words_a, words_b = transpose_x(xa), transpose_x(xb)
             if is_group(s - OUT_LAG):
                 store_score(s - OUT_LAG, out_bank)
-            if is_group(s):
-                xp_b = group_xp(b)
-            x_grouped = [(i, group_words(bank, False)) for i, bank in x_ahead]
+            if is_group(s + X_LEAD):
+                grouped_a = group_words(words_a, False)
 
             if is_group(s - 1):
                 multiply_tanh(b - GROUP)
             if is_group(s):
-                quantise_xp(b, xp_b)
+                quantise_xp(b)
             if is_group(s - 1):
                 fold_nodes(s - 1, 0)
-            for i, grouped in x_grouped[:1]:
-                quantise(grouped, *x_operand(i))
+            if is_group(s + X_LEAD):
+                quantise(grouped_a, *x_operand(xa))
             if is_group(s - 1):
                 fold_nodes(s - 1, 1)
 
@@ -259,15 +258,18 @@ def tile_bonsailayer_pa_t_kernel(tc, X, Z, W, V, th, out):
                 multiply_tanh(a)
             if is_group(s - 1):
                 fold_nodes(s - 1, 2)
-            for i, grouped in x_grouped[1:]:
-                quantise(grouped, *x_operand(i))
+            if is_group(s + X_LEAD):
+                quantise(group_words(words_b, False), *x_operand(xb))
             if is_group(s + XP_LEAD):
                 project(a + GROUP * XP_LEAD)
                 project(b + GROUP * XP_LEAD)
-                quantise_xp(a + GROUP * XP_LEAD, group_xp(a + GROUP * XP_LEAD))
+                group_xp(a + GROUP * XP_LEAD)
+                quantise_xp(a + GROUP * XP_LEAD)
             if is_group(s):
                 multiply_all_nodes(b)
                 tanh_nodes(b)
+            if is_group(s + XP_LEAD):
+                group_xp(b + GROUP * XP_LEAD)
 
         prob = keep.tile([P, NODES, SAMPLE_TILES], F32)
 
@@ -321,7 +323,7 @@ def tile_bonsailayer_pa_t_kernel(tc, X, Z, W, V, th, out):
             if pair == LOW_NODES:
                 for i in range(GROUP * XP_LEAD):
                     project(i)
-                xp_a = group_xp(0)
+                    group_xp(i)
                 path_probabilities()
             blocks = []
             for r in (2 * pair, 2 * pair + 1):
@@ -329,7 +331,7 @@ def tile_bonsailayer_pa_t_kernel(tc, X, Z, W, V, th, out):
             cols = slice(2 * pair * P, (2 * pair + 2) * P)
             head_unit(blocks, vw_codes[:, cols], vw_scales[:, cols])
         quantise(*waiting.pop(0))
-        quantise_xp(0, xp_a)
+        quantise_xp(0)
 
         for s in range(GROUPS + OUT_LAG):
             pipeline_step(s)

@@ -33,6 +33,7 @@ GROUPS = SAMPLE_TILES // GROUP
 X_LEAD = 2
 XP_LEAD = 1
 OUT_LAG = 2
+TAIL_GROUPS = 2
 
 FLOPS = 2 * PROJECTED * FEATURES * SAMPLES + 2 * 2 * NODES * CLASSES * PROJECTED * SAMPLES
 
@@ -45,6 +46,7 @@ def tile_bonsailayer_pa_t_kernel(tc, X, Z, W, V, th, out):
         codes_pool = ctx.enter_context(tc.tile_pool(name="codes", bufs=GROUP * (X_LEAD + 1)))
         work = ctx.enter_context(tc.tile_pool(name="work", bufs=3))
         product_pool = ctx.enter_context(tc.tile_pool(name="product", bufs=OUT_LAG + 2))
+        last_pool = ctx.enter_context(tc.tile_pool(name="last", bufs=GROUP * TAIL_GROUPS))
         words_psum = ctx.enter_context(tc.psum_pool(name="words_psum", bufs=2))
         xp_psum = ctx.enter_context(tc.psum_pool(name="xp_psum", bufs=2))
         nodes_psum = ctx.enter_context(tc.psum_pool(name="nodes_psum", bufs=1))
@@ -58,7 +60,7 @@ def tile_bonsailayer_pa_t_kernel(tc, X, Z, W, V, th, out):
         x_rows = []
         for g in range(SAMPLE_TILES // TILES_PER_LOAD):
             x_rows.append(keep.tile([P, TILES_PER_LOAD, FEATURES], BF16, name="x_rows%d" % g))
-        for j in range(TILES_PER_LOAD):
+        for j in range(GROUP):
             nc.sync.dma_start(out=x_rows[0][:, j, :], in_=x_loads[0][:, j, :])
         th_rows = keep.tile([P, P], BF16)
         nc.gpsimd.memset(th_rows[:], 0.0)
@@ -67,8 +69,13 @@ def tile_bonsailayer_pa_t_kernel(tc, X, Z, W, V, th, out):
             in_=th.rearrange("n (i p) -> (n i) p", p=P),
         )
         vw_rows = keep.tile([P, 2 * NODES, PROJECTED], BF16)
-        nc.sync.dma_start(out=vw_rows[:, 0:NODES, :], in_=V.rearrange("(n p) k -> p n k", p=P))
-        nc.sync.dma_start(out=vw_rows[:, NODES:, :], in_=W.rearrange("(n p) k -> p n k", p=P))
+        for first, rows in ((0, V), (NODES, W)):
+            loads = rows.rearrange("(n p) k -> p n k", p=P)
+            for n in range(0, NODES, 2):
+                end = min(n + 2, NODES)
+                nc.sync.dma_start(out=vw_rows[:, first + n : first + end, :], in_=loads[:, n:end, :])
+        for j in range(GROUP, TILES_PER_LOAD):
+            nc.sync.dma_start(out=x_rows[0][:, j, :], in_=x_loads[0][:, j, :])
         for g in range(1, SAMPLE_TILES // TILES_PER_LOAD):
             nc.sync.dma_start(out=x_rows[g][:], in_=x_loads[g])
 
@@ -221,6 +228,21 @@ def tile_bonsailayer_pa_t_kernel(tc, X, Z, W, V, th, out):
                 nc.tensor.transpose(bank[:, j, :], products[s][:, j, (NODES - 1) * CLASSES :], identity[:])
             return bank
 
+        def sum_while_transposing(i):
+            bank = xp_psum.tile([P, P], F32, tag="xp", name="sum_bank")
+            for n in range(NODES):
+                nc.tensor.matmul(
+                    out=bank[:],
+                    lhsT=products[i // GROUP][:, i % GROUP, n * CLASSES : (n + 1) * CLASSES],
+                    rhs=identity[:],
+                    is_transpose=True,
+                    start=(n == 0),
+                    stop=(n == NODES - 1),
+                )
+            last_sb = last_pool.tile([P, P], F32, tag="last_sb")
+            nc.scalar.copy(out=last_sb[:], in_=bank[:])
+            nc.sync.dma_start(out=out[:, i * P : (i + 1) * P], in_=last_sb[:])
+
         def store_score(s, bank):
             out_sb = work.tile([P, GROUP * P], F32, tag="out_sb")
             nc.scalar.copy(out=out_sb[:], in_=bank[:].rearrange("p j b -> p (j b)"))
@@ -229,14 +251,17 @@ def tile_bonsailayer_pa_t_kernel(tc, X, Z, W, V, th, out):
         def is_group(s):
             return 0 <= s < GROUPS
 
+        def is_folded(s):
+            return 0 <= s < GROUPS - TAIL_GROUPS
+
         def pipeline_step(s):
             a, b = GROUP * s, GROUP * s + 1
             xa, xb = a + GROUP * X_LEAD, b + GROUP * X_LEAD
-            if is_group(s - OUT_LAG):
+            if is_folded(s - OUT_LAG):
                 out_bank = transpose_score(s - OUT_LAG)
             if is_group(s + X_LEAD):
                 words_a, words_b = transpose_x(xa), transpose_x(xb)
-            if is_group(s - OUT_LAG):
+            if is_folded(s - OUT_LAG):
                 store_score(s - OUT_LAG, out_bank)
             if is_group(s + X_LEAD):
                 grouped_a = group_words(words_a, False)
@@ -245,19 +270,23 @@ def tile_bonsailayer_pa_t_kernel(tc, X, Z, W, V, th, out):
                 multiply_tanh(b - GROUP)
             if is_group(s):
                 quantise_xp(b)
-            if is_group(s - 1):
+            if is_folded(s - 1):
                 fold_nodes(s - 1, 0)
             if is_group(s + X_LEAD):
                 quantise(grouped_a, *x_operand(xa))
-            if is_group(s - 1):
+            if is_folded(s - 1):
                 fold_nodes(s - 1, 1)
 
             if is_group(s):
                 multiply_all_nodes(a)
                 tanh_nodes(a)
                 multiply_tanh(a)
-            if is_group(s - 1):
+            if is_group(s - 1) and not is_folded(s - 1):
+                sum_while_transposing(a - GROUP)
+                sum_while_transposing(b - GROUP)
+            if is_folded(s - 1):
                 fold_nodes(s - 1, 2)
+
             if is_group(s + X_LEAD):
                 quantise(group_words(words_b, False), *x_operand(xb))
             if is_group(s + XP_LEAD):
@@ -316,9 +345,12 @@ def tile_bonsailayer_pa_t_kernel(tc, X, Z, W, V, th, out):
         for t in range(PACK):
             cols = slice(t * X_PASSES * P, (t + 1) * X_PASSES * P)
             head_unit(pair_blocks(z_rows[:, t, :].bitcast(F32), X_PASSES), z_codes[:, cols], z_scales[:, cols])
-        for i in range(GROUP * X_LEAD):
-            codes, scales = x_operand(i)
-            head_unit(x_blocks(i), codes, scales)
+        def head_x(tiles):
+            for i in tiles:
+                codes, scales = x_operand(i)
+                head_unit(x_blocks(i), codes, scales)
+
+        head_x(range(GROUP))
         for pair in range(NODES):
             if pair == LOW_NODES:
                 for i in range(GROUP * XP_LEAD):
@@ -330,8 +362,10 @@ def tile_bonsailayer_pa_t_kernel(tc, X, Z, W, V, th, out):
                 blocks.extend(pair_blocks(vw_rows[:, r, :].bitcast(F32), 1))
             cols = slice(2 * pair * P, (2 * pair + 2) * P)
             head_unit(blocks, vw_codes[:, cols], vw_scales[:, cols])
+            if pair == LOW_NODES + 1:
+                quantise_xp(0)
+        head_x(range(GROUP, GROUP * X_LEAD))
         quantise(*waiting.pop(0))
-        quantise_xp(0)
 
-        for s in range(GROUPS + OUT_LAG):
+        for s in range(GROUPS + OUT_LAG - 1):
             pipeline_step(s)

@@ -32,7 +32,7 @@ GROUP = 2
 GROUPS = SAMPLE_TILES // GROUP
 X_LEAD = 2
 XP_LEAD = 1
-OUT_LAG = 2
+OUT_LAG = 3
 TAIL_GROUPS = 2
 
 FLOPS = 2 * PROJECTED * FEATURES * SAMPLES + 2 * 2 * NODES * CLASSES * PROJECTED * SAMPLES
@@ -218,7 +218,8 @@ def tile_bonsailayer_pa_t_kernel(tc, X, Z, W, V, th, out):
             first, count = FOLDS[f]
             low = slice(first * CLASSES, (first + count) * CLASSES)
             high = slice((first + count) * CLASSES, (first + 2 * count) * CLASSES)
-            nc.vector.tensor_tensor(
+            engine = nc.gpsimd if f in [2] else nc.vector
+            engine.tensor_tensor(
                 out=products[s][:, :, high], in0=products[s][:, :, low], in1=products[s][:, :, high], op=ALU.add
             )
 
@@ -274,8 +275,6 @@ def tile_bonsailayer_pa_t_kernel(tc, X, Z, W, V, th, out):
                 fold_nodes(s - 1, 0)
             if is_group(s + X_LEAD):
                 quantise(grouped_a, *x_operand(xa))
-            if is_folded(s - 1):
-                fold_nodes(s - 1, 1)
 
             if is_group(s):
                 multiply_all_nodes(a)
@@ -284,8 +283,6 @@ def tile_bonsailayer_pa_t_kernel(tc, X, Z, W, V, th, out):
             if is_group(s - 1) and not is_folded(s - 1):
                 sum_while_transposing(a - GROUP)
                 sum_while_transposing(b - GROUP)
-            if is_folded(s - 1):
-                fold_nodes(s - 1, 2)
 
             if is_group(s + X_LEAD):
                 quantise(group_words(words_b, False), *x_operand(xb))
@@ -294,6 +291,9 @@ def tile_bonsailayer_pa_t_kernel(tc, X, Z, W, V, th, out):
                 project(b + GROUP * XP_LEAD)
                 group_xp(a + GROUP * XP_LEAD)
                 quantise_xp(a + GROUP * XP_LEAD)
+            if is_folded(s - 1):
+                fold_nodes(s - 1, 1)
+                fold_nodes(s - 1, 2)
             if is_group(s):
                 multiply_all_nodes(b)
                 tanh_nodes(b)
@@ -367,5 +367,5 @@ def tile_bonsailayer_pa_t_kernel(tc, X, Z, W, V, th, out):
         head_x(range(GROUP, GROUP * X_LEAD))
         quantise(*waiting.pop(0))
 
-        for s in range(GROUPS + OUT_LAG - 1):
+        for s in range(GROUPS + OUT_LAG - TAIL_GROUPS):
             pipeline_step(s)

@@ -32,6 +32,7 @@ GROUP = 2
 GROUPS = SAMPLE_TILES // GROUP
 X_LEAD = 2
 XP_LEAD = 1
+SEPARATE_LEAD = 3
 OUT_LAG = 3
 TAIL_GROUPS = 2
 
@@ -110,7 +111,7 @@ def tile_bonsailayer_pa_t_kernel(tc, X, Z, W, V, th, out):
         vw_codes = keep.tile([P, 2 * NODES * P], U32, align_bytes=64)
         vw_scales = keep.tile([P, 2 * NODES * P], U8, align_bytes=64)
 
-        x_mx, xp_banks, xp_grouped, xp_mx, node_banks, products = {}, {}, {}, {}, {}, {}
+        x_separated, x_mx, xp_banks, xp_grouped, xp_mx, node_banks, products = {}, {}, {}, {}, {}, {}, {}
 
         def x_blocks(i):
             return pair_blocks(x_rows[i // TILES_PER_LOAD][:, i % TILES_PER_LOAD, :].bitcast(F32), X_PASSES)
@@ -121,9 +122,20 @@ def tile_bonsailayer_pa_t_kernel(tc, X, Z, W, V, th, out):
             x_mx[i] = (x_codes, x_scales)
             return x_codes[:], x_scales[:]
 
+        def separate_x(i):
+            separated = stage.tile([P, X_PASSES, 2, P], F32, tag="separated")
+            x_words = x_rows[i // TILES_PER_LOAD][:, i % TILES_PER_LOAD, :].bitcast(F32)
+            nc.vector.tensor_copy(
+                out=separated[:], in_=x_words.rearrange("p (c i u) -> p c u i", c=X_PASSES, u=2)
+            )
+            x_separated[i] = separated
+
         def transpose_x(i):
             bank = words_psum.tile([P, 2, 2, P], F32, tag="words")
-            transpose_blocks(bank, x_blocks(i))
+            if i in x_separated:
+                transpose_blocks(bank, [x_separated[i][:, c, u, :] for c in range(X_PASSES) for u in range(2)])
+            else:
+                transpose_blocks(bank, x_blocks(i))
             return bank
 
         def project(i):
@@ -214,13 +226,15 @@ def tile_bonsailayer_pa_t_kernel(tc, X, Z, W, V, th, out):
                     op1=ALU.mult,
                 )
 
-        def fold_nodes(s, f):
+        def fold_nodes(engine, s, tiles, f):
             first, count = FOLDS[f]
             low = slice(first * CLASSES, (first + count) * CLASSES)
             high = slice((first + count) * CLASSES, (first + 2 * count) * CLASSES)
-            engine = nc.gpsimd if f in [2] else nc.vector
             engine.tensor_tensor(
-                out=products[s][:, :, high], in0=products[s][:, :, low], in1=products[s][:, :, high], op=ALU.add
+                out=products[s][:, tiles, high],
+                in0=products[s][:, tiles, low],
+                in1=products[s][:, tiles, high],
+                op=ALU.add,
             )
 
         def transpose_score(s):
@@ -258,42 +272,52 @@ def tile_bonsailayer_pa_t_kernel(tc, X, Z, W, V, th, out):
         def pipeline_step(s):
             a, b = GROUP * s, GROUP * s + 1
             xa, xb = a + GROUP * X_LEAD, b + GROUP * X_LEAD
+            tile_a, tile_b, both = slice(0, 1), slice(1, 2), slice(0, GROUP)
             if is_folded(s - OUT_LAG):
                 out_bank = transpose_score(s - OUT_LAG)
             if is_group(s + X_LEAD):
                 words_a, words_b = transpose_x(xa), transpose_x(xb)
-            if is_folded(s - OUT_LAG):
-                store_score(s - OUT_LAG, out_bank)
             if is_group(s + X_LEAD):
                 grouped_a = group_words(words_a, False)
-
+            if is_folded(s - OUT_LAG):
+                store_score(s - OUT_LAG, out_bank)
             if is_group(s - 1):
                 multiply_tanh(b - GROUP)
+            if is_group(s + SEPARATE_LEAD):
+                separate_x(b + GROUP * SEPARATE_LEAD)
             if is_group(s):
                 quantise_xp(b)
-            if is_folded(s - 1):
-                fold_nodes(s - 1, 0)
             if is_group(s + X_LEAD):
                 quantise(grouped_a, *x_operand(xa))
-
+            if is_folded(s - 1):
+                fold_nodes(nc.vector, s - 1, tile_b, 0)
             if is_group(s):
                 multiply_all_nodes(a)
                 tanh_nodes(a)
+            if is_group(s):
                 multiply_tanh(a)
+            if is_folded(s - 1):
+                fold_nodes(nc.gpsimd, s - 1, tile_b, 1)
             if is_group(s - 1) and not is_folded(s - 1):
                 sum_while_transposing(a - GROUP)
                 sum_while_transposing(b - GROUP)
-
             if is_group(s + X_LEAD):
-                quantise(group_words(words_b, False), *x_operand(xb))
+                grouped_b = group_words(words_b, False)
+            if is_group(s + X_LEAD):
+                quantise(grouped_b, *x_operand(xb))
+            if is_folded(s - 1):
+                fold_nodes(nc.vector, s - 1, both, 2)
             if is_group(s + XP_LEAD):
                 project(a + GROUP * XP_LEAD)
                 project(b + GROUP * XP_LEAD)
+            if is_group(s + XP_LEAD):
                 group_xp(a + GROUP * XP_LEAD)
+            if is_group(s + XP_LEAD):
                 quantise_xp(a + GROUP * XP_LEAD)
-            if is_folded(s - 1):
-                fold_nodes(s - 1, 1)
-                fold_nodes(s - 1, 2)
+            if is_folded(s):
+                fold_nodes(nc.vector, s, tile_a, 0)
+            if is_folded(s):
+                fold_nodes(nc.gpsimd, s, tile_a, 1)
             if is_group(s):
                 multiply_all_nodes(b)
                 tanh_nodes(b)
@@ -367,5 +391,5 @@ def tile_bonsailayer_pa_t_kernel(tc, X, Z, W, V, th, out):
         head_x(range(GROUP, GROUP * X_LEAD))
         quantise(*waiting.pop(0))
 
-        for s in range(GROUPS + OUT_LAG - TAIL_GROUPS):
+        for s in range(GROUPS + 1):
             pipeline_step(s)

@@ -34,7 +34,6 @@ X_LEAD = 2
 XP_LEAD = 1
 SEPARATE_LEAD = 3
 OUT_LAG = 3
-TAIL_GROUPS = 2
 
 FLOPS = 2 * PROJECTED * FEATURES * SAMPLES + 2 * 2 * NODES * CLASSES * PROJECTED * SAMPLES
 
@@ -47,7 +46,7 @@ def tile_bonsailayer_pa_t_kernel(tc, X, Z, W, V, th, out):
         codes_pool = ctx.enter_context(tc.tile_pool(name="codes", bufs=GROUP * (X_LEAD + 1)))
         work = ctx.enter_context(tc.tile_pool(name="work", bufs=3))
         product_pool = ctx.enter_context(tc.tile_pool(name="product", bufs=OUT_LAG + 2))
-        last_pool = ctx.enter_context(tc.tile_pool(name="last", bufs=GROUP * TAIL_GROUPS))
+        last_pool = ctx.enter_context(tc.tile_pool(name="last", bufs=GROUP))
         words_psum = ctx.enter_context(tc.psum_pool(name="words_psum", bufs=2))
         xp_psum = ctx.enter_context(tc.psum_pool(name="xp_psum", bufs=2))
         nodes_psum = ctx.enter_context(tc.psum_pool(name="nodes_psum", bufs=1))
@@ -55,20 +54,21 @@ def tile_bonsailayer_pa_t_kernel(tc, X, Z, W, V, th, out):
 
         z_rows = keep.tile([P, PACK, FEATURES], BF16)
         z_loads = Z.rearrange("(p t) d -> p t d", t=PACK)
-        for t in range(PACK):
-            nc.sync.dma_start(out=z_rows[:, t, :], in_=z_loads[:, t, :])
+        for t, c in ((0, 0), (0, 1), (1, None), (2, None), (3, None)):
+            cols = slice(0, FEATURES) if c is None else slice(c * K_PASS, (c + 1) * K_PASS)
+            nc.sync.dma_start(out=z_rows[:, t, cols], in_=z_loads[:, t, cols])
         x_loads = X.rearrange("(g j p) d -> g p j d", j=TILES_PER_LOAD, p=P)
         x_rows = []
         for g in range(SAMPLE_TILES // TILES_PER_LOAD):
             x_rows.append(keep.tile([P, TILES_PER_LOAD, FEATURES], BF16, name="x_rows%d" % g))
-        for j in range(GROUP):
-            nc.sync.dma_start(out=x_rows[0][:, j, :], in_=x_loads[0][:, j, :])
         th_rows = keep.tile([P, P], BF16)
         nc.gpsimd.memset(th_rows[:], 0.0)
         nc.sync.dma_start(
             out=th_rows[0 : INTERNAL * SAMPLE_TILES, :],
             in_=th.rearrange("n (i p) -> (n i) p", p=P),
         )
+        for j in range(GROUP):
+            nc.sync.dma_start(out=x_rows[0][:, j, :], in_=x_loads[0][:, j, :])
         vw_rows = keep.tile([P, 2 * NODES, PROJECTED], BF16)
         for first, rows in ((0, V), (NODES, W)):
             loads = rows.rearrange("(n p) k -> p n k", p=P)
@@ -77,7 +77,9 @@ def tile_bonsailayer_pa_t_kernel(tc, X, Z, W, V, th, out):
                 nc.sync.dma_start(out=vw_rows[:, first + n : first + end, :], in_=loads[:, n:end, :])
         for j in range(GROUP, TILES_PER_LOAD):
             nc.sync.dma_start(out=x_rows[0][:, j, :], in_=x_loads[0][:, j, :])
-        for g in range(1, SAMPLE_TILES // TILES_PER_LOAD):
+        for j in range(0, TILES_PER_LOAD, GROUP):
+            nc.sync.dma_start(out=x_rows[1][:, j : j + GROUP, :], in_=x_loads[1][:, j : j + GROUP, :])
+        for g in range(2, SAMPLE_TILES // TILES_PER_LOAD):
             nc.sync.dma_start(out=x_rows[g][:], in_=x_loads[g])
 
         identity = keep.tile([P, P], F32)
@@ -244,7 +246,7 @@ def tile_bonsailayer_pa_t_kernel(tc, X, Z, W, V, th, out):
             return bank
 
         def sum_while_transposing(i):
-            bank = xp_psum.tile([P, P], F32, tag="xp", name="sum_bank")
+            bank = words_psum.tile([P, P], F32, tag="words", name="sum_bank")
             for n in range(NODES):
                 nc.tensor.matmul(
                     out=bank[:],
@@ -267,20 +269,20 @@ def tile_bonsailayer_pa_t_kernel(tc, X, Z, W, V, th, out):
             return 0 <= s < GROUPS
 
         def is_folded(s):
-            return 0 <= s < GROUPS - TAIL_GROUPS
+            return 0 <= s < GROUPS - 1
 
         def pipeline_step(s):
             a, b = GROUP * s, GROUP * s + 1
             xa, xb = a + GROUP * X_LEAD, b + GROUP * X_LEAD
             tile_a, tile_b, both = slice(0, 1), slice(1, 2), slice(0, GROUP)
-            if is_folded(s - OUT_LAG):
-                out_bank = transpose_score(s - OUT_LAG)
+            out_groups = range(s - OUT_LAG, s - OUT_LAG + 1 if s < GROUPS else GROUPS - 1)
+            out_banks = [(g, transpose_score(g)) for g in out_groups if is_folded(g)]
             if is_group(s + X_LEAD):
                 words_a, words_b = transpose_x(xa), transpose_x(xb)
             if is_group(s + X_LEAD):
                 grouped_a = group_words(words_a, False)
-            if is_folded(s - OUT_LAG):
-                store_score(s - OUT_LAG, out_bank)
+            for g, bank in out_banks:
+                store_score(g, bank)
             if is_group(s - 1):
                 multiply_tanh(b - GROUP)
             if is_group(s + SEPARATE_LEAD):
@@ -298,7 +300,7 @@ def tile_bonsailayer_pa_t_kernel(tc, X, Z, W, V, th, out):
                 multiply_tanh(a)
             if is_folded(s - 1):
                 fold_nodes(nc.gpsimd, s - 1, tile_b, 1)
-            if is_group(s - 1) and not is_folded(s - 1):
+            if s == GROUPS:
                 sum_while_transposing(a - GROUP)
                 sum_while_transposing(b - GROUP)
             if is_group(s + X_LEAD):
@@ -331,18 +333,16 @@ def tile_bonsailayer_pa_t_kernel(tc, X, Z, W, V, th, out):
             nc.gpsimd.tensor_copy(out=th_f32[:], in_=th_rows[:])
             th_bank = words_psum.tile([P, P], F32, tag="words")
             nc.tensor.transpose(th_bank[:], th_f32[:], identity[:])
-            th_cols = keep.tile([P, INTERNAL, SAMPLE_TILES], F32)
-            nc.scalar.copy(
-                out=th_cols[:].rearrange("p n i -> p (n i)"), in_=th_bank[:, 0 : INTERNAL * SAMPLE_TILES]
-            )
             go_left = keep.tile([P, INTERNAL, SAMPLE_TILES], F32)
             go_right = keep.tile([P, INTERNAL, SAMPLE_TILES], F32)
-            nc.gpsimd.tensor_scalar(
-                out=go_left[:], in0=th_cols[:], scalar1=0.5, scalar2=0.5, op0=ALU.mult, op1=ALU.add
-            )
-            nc.gpsimd.tensor_scalar(
-                out=go_right[:], in0=th_cols[:], scalar1=-0.5, scalar2=0.5, op0=ALU.mult, op1=ALU.add
-            )
+            for go, half in ((go_left, 0.5), (go_right, -0.5)):
+                nc.scalar.activation(
+                    out=go[:].rearrange("p n i -> p (n i)"),
+                    in_=th_bank[:, 0 : INTERNAL * SAMPLE_TILES],
+                    func=ACT.Copy,
+                    scale=half,
+                    bias=0.5,
+                )
             nc.gpsimd.memset(prob[:, 0, :], 1.0)
             for n in range(INTERNAL):
                 nc.gpsimd.tensor_tensor(
@@ -372,20 +372,27 @@ def tile_bonsailayer_pa_t_kernel(tc, X, Z, W, V, th, out):
         def head_x(tiles):
             for i in tiles:
                 codes, scales = x_operand(i)
-                head_unit(x_blocks(i), codes, scales)
+                if i in x_separated:
+                    blocks = [x_separated[i][:, c, u, :] for c in range(X_PASSES) for u in range(2)]
+                else:
+                    blocks = x_blocks(i)
+                head_unit(blocks, codes, scales)
 
         head_x(range(GROUP))
+        path_probabilities()
         for pair in range(NODES):
             if pair == LOW_NODES:
                 for i in range(GROUP * XP_LEAD):
                     project(i)
                     group_xp(i)
-                path_probabilities()
             blocks = []
             for r in (2 * pair, 2 * pair + 1):
                 blocks.extend(pair_blocks(vw_rows[:, r, :].bitcast(F32), 1))
             cols = slice(2 * pair * P, (2 * pair + 2) * P)
             head_unit(blocks, vw_codes[:, cols], vw_scales[:, cols])
+            if pair == LOW_NODES:
+                separate_x(2)
+                separate_x(3)
             if pair == LOW_NODES + 1:
                 quantise_xp(0)
         head_x(range(GROUP, GROUP * X_LEAD))

@@ -381,21 +381,19 @@ def tile_bonsailayer_pa_t_kernel(tc, X, Z, W, V, th, out):
         head_x(range(GROUP))
         path_probabilities()
         for pair in range(NODES):
-            if pair == LOW_NODES:
-                for i in range(GROUP * XP_LEAD):
-                    project(i)
-                    group_xp(i)
             blocks = []
             for r in (2 * pair, 2 * pair + 1):
                 blocks.extend(pair_blocks(vw_rows[:, r, :].bitcast(F32), 1))
             cols = slice(2 * pair * P, (2 * pair + 2) * P)
             head_unit(blocks, vw_codes[:, cols], vw_scales[:, cols])
-            if pair == LOW_NODES:
-                separate_x(2)
-                separate_x(3)
-            if pair == LOW_NODES + 1:
-                quantise_xp(0)
-        head_x(range(GROUP, GROUP * X_LEAD))
+            if pair == NODES - 2:
+                project(0)
+                group_xp(0)
+        head_x([2])
+        quantise_xp(0)
+        head_x([3])
+        project(1)
+        group_xp(1)
         quantise(*waiting.pop(0))
 
         for s in range(GROUPS + 1):

from contextlib import ExitStack

import concourse.mybir as mybir
from concourse.masks import make_identity

F32 = mybir.dt.float32
BF16 = mybir.dt.bfloat16
U32 = mybir.dt.uint32
U8 = mybir.dt.uint8
FP8X4 = mybir.dt.float8_e4m3fn_x4
ACT = mybir.ActivationFunctionType
ALU = mybir.AluOpType

P = 128
PACK = 4
K_PASS = P * PACK
BANK = 512

SAMPLES, FEATURES, PROJECTED, CLASSES = 4096, 1024, 512, 128
INTERNAL, NODES = 3, 7
SAMPLE_TILES = SAMPLES // P
TILES_PER_LOAD = 4
X_PASSES = FEATURES // K_PASS
LOW_NODES = BANK // CLASSES

LOW_WIDTHS = (512,)
HIGH_WIDTHS = (256, 128)

FOLDS = ((0, 3), (3, 2), (5, 1))

GROUP = 2
GROUPS = SAMPLE_TILES // GROUP
X_LEAD = 2
XP_LEAD = 1
SEPARATE_LEAD = 3
OUT_LAG = 3

FLOPS = 2 * PROJECTED * FEATURES * SAMPLES + 2 * 2 * NODES * CLASSES * PROJECTED * SAMPLES


def tile_bonsailayer_pa_t_kernel(tc, X, Z, W, V, th, out):
    nc = tc.nc
    with ExitStack() as ctx:
        keep = ctx.enter_context(tc.tile_pool(name="keep", bufs=1))
        stage = ctx.enter_context(tc.tile_pool(name="stage", bufs=3))
        codes_pool = ctx.enter_context(tc.tile_pool(name="codes", bufs=GROUP * (X_LEAD + 1)))
        work = ctx.enter_context(tc.tile_pool(name="work", bufs=3))
        product_pool = ctx.enter_context(tc.tile_pool(name="product", bufs=OUT_LAG + 2))
        last_pool = ctx.enter_context(tc.tile_pool(name="last", bufs=GROUP))
        words_psum = ctx.enter_context(tc.psum_pool(name="words_psum", bufs=2))
        xp_psum = ctx.enter_context(tc.psum_pool(name="xp_psum", bufs=2))
        nodes_psum = ctx.enter_context(tc.psum_pool(name="nodes_psum", bufs=1))
        ctx.enter_context(tc.manual_schedule())

        z_rows = keep.tile([P, PACK, FEATURES], BF16)
        z_loads = Z.rearrange("(p t) d -> p t d", t=PACK)
        for t, c in ((0, 0), (0, 1), (1, None), (2, None), (3, None)):
            cols = slice(0, FEATURES) if c is None else slice(c * K_PASS, (c + 1) * K_PASS)
            nc.sync.dma_start(out=z_rows[:, t, cols], in_=z_loads[:, t, cols])
        x_loads = X.rearrange("(g j p) d -> g p j d", j=TILES_PER_LOAD, p=P)
        x_rows = []
        for g in range(SAMPLE_TILES // TILES_PER_LOAD):
            x_rows.append(keep.tile([P, TILES_PER_LOAD, FEATURES], BF16, name="x_rows%d" % g))
        th_rows = keep.tile([P, P], BF16)
        nc.gpsimd.memset(th_rows[:], 0.0)
        nc.sync.dma_start(
            out=th_rows[0 : INTERNAL * SAMPLE_TILES, :],
            in_=th.rearrange("n (i p) -> (n i) p", p=P),
        )
        for j in range(GROUP):
            nc.sync.dma_start(out=x_rows[0][:, j, :], in_=x_loads[0][:, j, :])
        vw_rows = keep.tile([P, 2 * NODES, PROJECTED], BF16)
        for first, rows in ((0, V), (NODES, W)):
            loads = rows.rearrange("(n p) k -> p n k", p=P)
            for n in range(0, NODES, 2):
                end = min(n + 2, NODES)
                nc.sync.dma_start(out=vw_rows[:, first + n : first + end, :], in_=loads[:, n:end, :])
        for j in range(GROUP, TILES_PER_LOAD):
            nc.sync.dma_start(out=x_rows[0][:, j, :], in_=x_loads[0][:, j, :])
        for j in range(0, TILES_PER_LOAD, GROUP):
            nc.sync.dma_start(out=x_rows[1][:, j : j + GROUP, :], in_=x_loads[1][:, j : j + GROUP, :])
        for g in range(2, SAMPLE_TILES // TILES_PER_LOAD):
            nc.sync.dma_start(out=x_rows[g][:], in_=x_loads[g])

        identity = keep.tile([P, P], F32)
        make_identity(nc, identity[:])
        warm = keep.tile([P, 1], F32)
        nc.vector.memset(warm[:], 0.0)
        nc.scalar.activation(out=warm[:], in_=warm[:], func=ACT.Tanh)

        def pair_blocks(words, passes):
            return [words[:, 2 * P * c + u : 2 * P * (c + 1) : 2] for c in range(passes) for u in range(2)]

        def transpose_blocks(bank, blocks):
            for slot in range(2):
                for u in range(2):
                    nc.tensor.transpose(bank[:, slot, u, :], blocks[2 * slot + u], identity[:])

        def group_words(bank, on_vector):
            grouped = stage.tile([P, 2 * P * PACK], BF16, tag="grouped", align_bytes=64)
            copy = nc.vector.tensor_copy if on_vector else nc.scalar.copy
            copy(
                out=grouped[:].bitcast(F32).rearrange("p (s r u) -> p s r u", s=2, u=2),
                in_=bank[:].rearrange("p s u r -> p s r u"),
            )
            return grouped

        def quantise(grouped, codes, scales):
            nc.vector.quantize_mx(out=codes.bitcast(FP8X4), scales=scales, in_=grouped[:])

        z_codes = keep.tile([P, PACK * X_PASSES * P], U32, align_bytes=64)
        z_scales = keep.tile([P, PACK * X_PASSES * P], U8, align_bytes=64)
        vw_codes = keep.tile([P, 2 * NODES * P], U32, align_bytes=64)
        vw_scales = keep.tile([P, 2 * NODES * P], U8, align_bytes=64)

        x_separated, x_mx, xp_banks, xp_grouped, xp_mx, node_banks, products = {}, {}, {}, {}, {}, {}, {}

        def x_blocks(i):
            return pair_blocks(x_rows[i // TILES_PER_LOAD][:, i % TILES_PER_LOAD, :].bitcast(F32), X_PASSES)

        def x_operand(i):
            x_codes = codes_pool.tile([P, X_PASSES * P], U32, tag="x_codes", align_bytes=64)
            x_scales = codes_pool.tile([P, X_PASSES * P], U8, tag="x_scales", align_bytes=64)
            x_mx[i] = (x_codes, x_scales)
            return x_codes[:], x_scales[:]

        def separate_x(i):
            separated = stage.tile([P, X_PASSES, 2, P], F32, tag="separated")
            x_words = x_rows[i // TILES_PER_LOAD][:, i % TILES_PER_LOAD, :].bitcast(F32)
            nc.vector.tensor_copy(
                out=separated[:], in_=x_words.rearrange("p (c i u) -> p c u i", c=X_PASSES, u=2)
            )
            x_separated[i] = separated

        def transpose_x(i):
            bank = words_psum.tile([P, 2, 2, P], F32, tag="words")
            if i in x_separated:
                transpose_blocks(bank, [x_separated[i][:, c, u, :] for c in range(X_PASSES) for u in range(2)])
            else:
                transpose_blocks(bank, x_blocks(i))
            return bank

        def project(i):
            x_codes, x_scales = x_mx[i]
            bank = xp_psum.tile([P, PACK, P], F32, tag="xp")
            for t in range(PACK):
                for c in range(X_PASSES):
                    z_cols = slice((t * X_PASSES + c) * P, (t * X_PASSES + c + 1) * P)
                    x_cols = slice(c * P, (c + 1) * P)
                    nc.tensor.matmul_mx(
                        out=bank[:, t, :],
                        lhsT=z_codes[:, z_cols].bitcast(FP8X4),
                        lhsT_scale=z_scales[:, z_cols],
                        rhs=x_codes[:, x_cols].bitcast(FP8X4),
                        rhs_scale=x_scales[:, x_cols],
                        start=(c == 0),
                        stop=(c == X_PASSES - 1),
                    )
            xp_banks[i] = bank

        def group_xp(i):
            grouped = stage.tile([P, P, PACK], BF16, tag="xp_grouped", align_bytes=64)
            nc.scalar.activation(
                out=grouped[:], in_=xp_banks[i][:].rearrange("p t b -> p b t"), func=ACT.Copy, scale=1.0 / PROJECTED
            )
            xp_grouped[i] = grouped

        def quantise_xp(i):
            xp_codes = codes_pool.tile([P, P], U32, tag="xp_codes", align_bytes=64)
            xp_scales = codes_pool.tile([P, P], U8, tag="xp_scales", align_bytes=64)
            nc.vector.quantize_mx(
                out=xp_codes[:].bitcast(FP8X4), scales=xp_scales[:], in_=xp_grouped[i][:].rearrange("p b t -> p (b t)")
            )
            xp_mx[i] = (xp_codes, xp_scales)

        def multiply_nodes(bank, i, first_row_tile, widths):
            xp_codes, xp_scales = xp_mx[i]
            done = 0
            for width in widths:
                vw_cols = slice(first_row_tile * P + done, first_row_tile * P + done + width)
                nc.tensor.matmul_mx(
                    out=bank[:, done : done + width],
                    lhsT=xp_codes[:].bitcast(FP8X4),
                    lhsT_scale=xp_scales[:],
                    rhs=vw_codes[:, vw_cols].bitcast(FP8X4),
                    rhs_scale=vw_scales[:, vw_cols],
                    start=True,
                    stop=True,
                )
                done += width

        def multiply_all_nodes(i):
            vx_low = nodes_psum.tile([P, BANK], F32, tag="vx_low")
            vx_high = nodes_psum.tile([P, BANK], F32, tag="vx_high")
            wx_low = nodes_psum.tile([P, BANK], F32, tag="wx_low")
            wx_high = nodes_psum.tile([P, BANK], F32, tag="wx_high")
            multiply_nodes(vx_low, i, 0, LOW_WIDTHS)
            multiply_nodes(vx_high, i, LOW_NODES, HIGH_WIDTHS)
            multiply_nodes(wx_low, i, NODES, LOW_WIDTHS)
            multiply_nodes(wx_high, i, NODES + LOW_NODES, HIGH_WIDTHS)
            node_banks[i] = (vx_low, vx_high, wx_low, wx_high)

        def tanh_nodes(i):
            vx_low, vx_high, wx_low, wx_high = node_banks[i]
            tanh_vx = work.tile([P, NODES * CLASSES], F32, tag="tanh_vx")
            nc.scalar.activation(out=tanh_vx[:, 0:BANK], in_=vx_low[:], func=ACT.Tanh)
            nc.scalar.activation(
                out=tanh_vx[:, BANK:], in_=vx_high[:, 0 : NODES * CLASSES - BANK], func=ACT.Tanh
            )
            node_banks[i] = (tanh_vx, wx_low, wx_high)

        def multiply_tanh(i):
            tanh_vx, wx_low, wx_high = node_banks[i]
            s, j = divmod(i, GROUP)
            if j == 0:
                product = product_pool.tile([P, GROUP, NODES * CLASSES], F32, tag="product")
                products[s] = product
            for n in range(NODES):
                wx = wx_low if n < LOW_NODES else wx_high
                bank_cols = slice((n % LOW_NODES) * CLASSES, (n % LOW_NODES + 1) * CLASSES)
                node_cols = slice(n * CLASSES, (n + 1) * CLASSES)
                nc.vector.scalar_tensor_tensor(
                    out=products[s][:, j, node_cols],
                    in0=wx[:, bank_cols],
                    scalar=prob[:, n, i : i + 1],
                    in1=tanh_vx[:, node_cols],
                    op0=ALU.mult,
                    op1=ALU.mult,
                )

        def fold_nodes(engine, s, tiles, f):
            first, count = FOLDS[f]
            low = slice(first * CLASSES, (first + count) * CLASSES)
            high = slice((first + count) * CLASSES, (first + 2 * count) * CLASSES)
            engine.tensor_tensor(
                out=products[s][:, tiles, high],
                in0=products[s][:, tiles, low],
                in1=products[s][:, tiles, high],
                op=ALU.add,
            )

        def transpose_score(s):
            bank = xp_psum.tile([P, GROUP, P], F32, tag="xp", name="out_bank")
            for j in range(GROUP):
                nc.tensor.transpose(bank[:, j, :], products[s][:, j, (NODES - 1) * CLASSES :], identity[:])
            return bank

        def sum_while_transposing(i):
            bank = words_psum.tile([P, P], F32, tag="words", name="sum_bank")
            for n in range(NODES):
                nc.tensor.matmul(
                    out=bank[:],
                    lhsT=products[i // GROUP][:, i % GROUP, n * CLASSES : (n + 1) * CLASSES],
                    rhs=identity[:],
                    is_transpose=True,
                    start=(n == 0),
                    stop=(n == NODES - 1),
                )
            last_sb = last_pool.tile([P, P], F32, tag="last_sb")
            nc.scalar.copy(out=last_sb[:], in_=bank[:])
            nc.sync.dma_start(out=out[:, i * P : (i + 1) * P], in_=last_sb[:])

        def store_score(s, bank):
            out_sb = work.tile([P, GROUP * P], F32, tag="out_sb")
            nc.scalar.copy(out=out_sb[:], in_=bank[:].rearrange("p j b -> p (j b)"))
            nc.sync.dma_start(out=out[:, s * GROUP * P : (s + 1) * GROUP * P], in_=out_sb[:])

        def is_group(s):
            return 0 <= s < GROUPS

        def is_folded(s):
            return 0 <= s < GROUPS - 1

        def pipeline_step(s):
            a, b = GROUP * s, GROUP * s + 1
            xa, xb = a + GROUP * X_LEAD, b + GROUP * X_LEAD
            tile_a, tile_b, both = slice(0, 1), slice(1, 2), slice(0, GROUP)
            out_groups = range(s - OUT_LAG, s - OUT_LAG + 1 if s < GROUPS else GROUPS - 1)
            out_banks = [(g, transpose_score(g)) for g in out_groups if is_folded(g)]
            if is_group(s + X_LEAD):
                words_a, words_b = transpose_x(xa), transpose_x(xb)
            if is_group(s + X_LEAD):
                grouped_a = group_words(words_a, False)
            for g, bank in out_banks:
                store_score(g, bank)
            if is_group(s - 1):
                multiply_tanh(b - GROUP)
            if is_group(s + SEPARATE_LEAD):
                separate_x(b + GROUP * SEPARATE_LEAD)
            if is_group(s):
                quantise_xp(b)
            if is_group(s + X_LEAD):
                quantise(grouped_a, *x_operand(xa))
            if is_folded(s - 1):
                fold_nodes(nc.vector, s - 1, tile_b, 0)
            if is_group(s):
                multiply_all_nodes(a)
                tanh_nodes(a)
            if is_group(s):
                multiply_tanh(a)
            if is_folded(s - 1):
                fold_nodes(nc.gpsimd, s - 1, tile_b, 1)
            if s == GROUPS:
                sum_while_transposing(a - GROUP)
                sum_while_transposing(b - GROUP)
            if is_group(s + X_LEAD):
                grouped_b = group_words(words_b, False)
            if is_group(s + X_LEAD):
                quantise(grouped_b, *x_operand(xb))
            if is_folded(s - 1):
                fold_nodes(nc.vector, s - 1, both, 2)
            if is_group(s + XP_LEAD):
                project(a + GROUP * XP_LEAD)
                project(b + GROUP * XP_LEAD)
            if is_group(s + XP_LEAD):
                group_xp(a + GROUP * XP_LEAD)
            if is_group(s + XP_LEAD):
                quantise_xp(a + GROUP * XP_LEAD)
            if is_folded(s):
                fold_nodes(nc.vector, s, tile_a, 0)
            if is_folded(s):
                fold_nodes(nc.gpsimd, s, tile_a, 1)
            if is_group(s):
                multiply_all_nodes(b)
                tanh_nodes(b)
            if is_group(s + XP_LEAD):
                group_xp(b + GROUP * XP_LEAD)

        prob = keep.tile([P, NODES, SAMPLE_TILES], F32)

        def path_probabilities():
            th_f32 = keep.tile([P, P], F32)
            nc.gpsimd.tensor_copy(out=th_f32[:], in_=th_rows[:])
            th_bank = words_psum.tile([P, P], F32, tag="words")
            nc.tensor.transpose(th_bank[:], th_f32[:], identity[:])
            go_left = keep.tile([P, INTERNAL, SAMPLE_TILES], F32)
            go_right = keep.tile([P, INTERNAL, SAMPLE_TILES], F32)
            for go, half in ((go_left, 0.5), (go_right, -0.5)):
                nc.scalar.activation(
                    out=go[:].rearrange("p n i -> p (n i)"),
                    in_=th_bank[:, 0 : INTERNAL * SAMPLE_TILES],
                    func=ACT.Copy,
                    scale=half,
                    bias=0.5,
                )
            nc.gpsimd.memset(prob[:, 0, :], 1.0)
            for n in range(INTERNAL):
                nc.gpsimd.tensor_tensor(
                    out=prob[:, 2 * n + 1, :], in0=prob[:, n, :], in1=go_left[:, n, :], op=ALU.mult
                )
                nc.gpsimd.tensor_tensor(
                    out=prob[:, 2 * n + 2, :], in0=prob[:, n, :], in1=go_right[:, n, :], op=ALU.mult
                )

        head_banks = [(words_psum, "words"), (nodes_psum, "vx_low"), (nodes_psum, "vx_high"), (words_psum, "words"), (nodes_psum, "wx_low"), (nodes_psum, "wx_high")]
        units_done = []
        waiting = []

        def head_unit(blocks, codes, scales):
            n = len(units_done)
            units_done.append(n)
            pool, tag = head_banks[n % 6]
            bank = pool.tile([P, 2, 2, P], F32, tag=tag, name="head_bank")
            transpose_blocks(bank, blocks)
            waiting.append((group_words(bank, n % 3 == 2), codes, scales))
            if len(waiting) > 1:
                quantise(*waiting.pop(0))

        for t in range(PACK):
            cols = slice(t * X_PASSES * P, (t + 1) * X_PASSES * P)
            head_unit(pair_blocks(z_rows[:, t, :].bitcast(F32), X_PASSES), z_codes[:, cols], z_scales[:, cols])
        def head_x(tiles):
            for i in tiles:
                codes, scales = x_operand(i)
                if i in x_separated:
                    blocks = [x_separated[i][:, c, u, :] for c in range(X_PASSES) for u in range(2)]
                else:
                    blocks = x_blocks(i)
                head_unit(blocks, codes, scales)

        head_x(range(GROUP))
        path_probabilities()
        for pair in range(NODES):
            blocks = []
            for r in (2 * pair, 2 * pair + 1):
                blocks.extend(pair_blocks(vw_rows[:, r, :].bitcast(F32), 1))
            cols = slice(2 * pair * P, (2 * pair + 2) * P)
            head_unit(blocks, vw_codes[:, cols], vw_scales[:, cols])
            if pair == NODES - 2:
                project(0)
                group_xp(0)
        head_x([2])
        quantise_xp(0)
        head_x([3])
        project(1)
        group_xp(1)
        quantise(*waiting.pop(0))

        for s in range(GROUPS + 1):
            pipeline_step(s)
